import numpy as np
import ml_dtypes


def mxq(x, axis, fmt="e4m3"):
    dtype, down = {"e4m3": (ml_dtypes.float8_e4m3fn, 7), "e5m2": (ml_dtypes.float8_e5m2, 14)}[fmt]
    v = np.moveaxis(np.asarray(x, np.float32).astype(ml_dtypes.bfloat16).astype(np.float64), axis, -1)
    blocks = v.reshape(v.shape[:-1] + (-1, 32))
    amax = np.abs(blocks).max(-1, keepdims=True)
    byte = np.maximum(np.where(amax > 0, np.frexp(amax)[1] - 1 + 127, 0) - down, 1)
    scale = np.exp2(byte - 127.0)
    codes = (blocks / scale).astype(np.float32).astype(dtype).astype(np.float64)
    return np.moveaxis((codes * scale).reshape(v.shape), -1, axis)


WIDE = False


def mx_kscale(k):
    if not WIDE:
        return np.ones(k)
    levels = np.array([10, -10, 5, -5, 0])
    a = np.random.permutation(np.resize(levels, k // 512 * 4)).reshape(k // 512, 4)
    idx = np.arange(k)
    return np.exp2(a[idx // 512, idx % 128 // 32])


BF16 = ml_dtypes.bfloat16


def bf(x):
    return np.asarray(x, np.float32).astype(BF16)


def f64(x):
    return np.asarray(x).astype(np.float64)


B, S, H, I, R = 4, 64, 2048, 7168, 512
EPS = 1e-05


def rmsnorm(h, w):
    var = np.mean(h * h, axis=-1, keepdims=True)
    return h * (1.0 / np.sqrt(var + EPS)) * w


def silu(v):
    return v / (1.0 + np.exp(-v))


def setup_inputs():
    s, t = mx_kscale(H), mx_kscale(R)
    return {"x": bf(np.random.standard_normal((B, S, H))),
            "residual": bf(np.random.standard_normal((B, S, H))),
            "ln_w": bf((1.0 + 0.1 * np.random.standard_normal(H)) * s),
            "w_gate_v": bf(np.random.standard_normal((H, R)) / np.sqrt(H) / s[:, None] * t),
            "w_gate_u": bf(np.random.standard_normal((R, I)) / np.sqrt(R) / t[:, None]),
            "w_up_v": bf(np.random.standard_normal((H, R)) / np.sqrt(H) / s[:, None] * t),
            "w_up_u": bf(np.random.standard_normal((R, I)) / np.sqrt(R) / t[:, None])}


def reference(x, residual, ln_w, w_gate_v, w_gate_u, w_up_v, w_up_u):
    h = f64(x) + f64(residual)
    n = rmsnorm(h, f64(ln_w))
    nq = mxq(n, 2, "e4m3")
    gate_r = nq @ mxq(f64(w_gate_v), 0, "e4m3")
    up_r = nq @ mxq(f64(w_up_v), 0, "e4m3")
    gate = silu(mxq(gate_r, 2, "e4m3") @ mxq(f64(w_gate_u), 0, "e4m3"))
    up = mxq(up_r, 2, "e4m3") @ mxq(f64(w_up_u), 0, "e4m3")
    return gate * up

@@ -1,0 +1,307 @@
+from contextlib import ExitStack
+
+import concourse.mybir as mybir
+from concourse.masks import make_identity
+
+F32 = mybir.dt.float32
+BF16 = mybir.dt.bfloat16
+U32 = mybir.dt.uint32
+U8 = mybir.dt.uint8
+FP8X4 = mybir.dt.float8_e4m3fn_x4
+ACT = mybir.ActivationFunctionType
+ALU = mybir.AluOpType
+
+P = 128
+PACK = 4
+K_PASS = P * PACK
+TOKENS = 256
+TOKEN_TILES = TOKENS // P
+H = 2048
+H_PASSES = H // K_PASS
+R = 512
+I = 7168
+EPS = 1e-05
+BANK = 512
+HALF = 512
+PIECE = 2 * HALF
+BANKS_PER_PIECE = PIECE // BANK
+V_PIECES = H_PASSES * R // PIECE
+U_PIECES = I // PIECE
+RUN = 4
+GATE = 0
+UP = 1
+LOADS_AHEAD = 5
+
+FLOPS = 2 * TOKENS * (2 * H * R + 2 * R * I)
+
+
+def tile_neuronllamamlp_pa_kernel(
+    tc, x, residual, ln_w, w_gate_v, w_gate_u, w_up_v, w_up_u, out
+):
+    nc = tc.nc
+    x_rows = x.flatten_outer_dims()
+    res_rows = residual.flatten_outer_dims()
+    out_rows = out.flatten_outer_dims()
+    v_views = [w.rearrange("(g j p) r -> p g j r", j=PACK, p=P) for w in (w_gate_v, w_up_v)]
+    u_views = [w.rearrange("(j p) i -> p j i", p=P) for w in (w_gate_u, w_up_u)]
+    regroup_copy = (nc.vector.tensor_copy, nc.scalar.copy)
+
+    with ExitStack() as ctx:
+        const = ctx.enter_context(tc.tile_pool(name="const", bufs=1))
+        keep = ctx.enter_context(tc.tile_pool(name="keep", bufs=1))
+        small = ctx.enter_context(tc.tile_pool(name="small", bufs=2))
+        raw_pool = ctx.enter_context(tc.tile_pool(name="raw", bufs=12))
+        grouped_pool = ctx.enter_context(tc.tile_pool(name="grouped", bufs=4))
+        u_pool = ctx.enter_context(tc.tile_pool(name="u_codes", bufs=4))
+        act_pool = ctx.enter_context(tc.tile_pool(name="gate_act", bufs=3))
+        product_pool = ctx.enter_context(tc.tile_pool(name="product", bufs=4))
+        psum = ctx.enter_context(tc.psum_pool(name="psum", bufs=8))
+        ctx.enter_context(tc.manual_schedule())
+
+        n_grouped = keep.tile([P, TOKEN_TILES, H_PASSES, P, PACK], BF16, align_bytes=64)
+        n_codes = keep.tile([P, TOKEN_TILES, H_PASSES, P], U32, align_bytes=64)
+        n_scales = keep.tile([P, TOKEN_TILES, H_PASSES, P], U8, align_bytes=64)
+        v_codes = [
+            keep.tile([P, H_PASSES, R], U32, align_bytes=64, name="v_codes%d" % m)
+            for m in (GATE, UP)
+        ]
+        v_scales = [
+            keep.tile([P, H_PASSES, R], U8, align_bytes=64, name="v_scales%d" % m)
+            for m in (GATE, UP)
+        ]
+        r_grouped = keep.tile([P, 2, TOKEN_TILES, P, PACK], BF16, align_bytes=64)
+        r_codes = keep.tile([P, 2, TOKEN_TILES, P], U32, align_bytes=64)
+        r_scales = keep.tile([P, 2, TOKEN_TILES, P], U8, align_bytes=64)
+
+        x_res, h, h_scaled, rms, rstd, h_t = {}, {}, {}, {}, {}, {}
+        raw_halves, grouped, u_codes, u_scales = {}, {}, {}, {}
+        r_t, banks, gate_act, product = {}, {}, {}, {}
+
+        def load_tokens(tt):
+            rows = slice(tt * P, (tt + 1) * P)
+            x_res[tt] = raw_pool.tile([P, 2, H], BF16, tag="raw", name="x_res")
+            nc.sync.dma_start(out=x_res[tt][:, 0, :], in_=x_rows[rows, :])
+            nc.sync.dma_start(out=x_res[tt][:, 1, :], in_=res_rows[rows, :])
+
+        def add_residual(tt):
+            h[tt] = raw_pool.tile([P, H], F32, tag="raw", name="h")
+            nc.vector.tensor_tensor(
+                out=h[tt][:], in0=x_res[tt][:, 0, :], in1=x_res[tt][:, 1, :], op=ALU.add
+            )
+
+        def root_mean_square(tt):
+            h_scaled[tt] = raw_pool.tile([P, H], F32, tag="raw", name="h_scaled")
+            sum_sq = small.tile([P, 1], F32, name="sum_sq")
+            nc.scalar.activation(
+                out=h_scaled[tt][:], in_=h[tt][:], func=ACT.Square, accum_out=sum_sq[:]
+            )
+            rms[tt] = small.tile([P, 1], F32, name="rms")
+            nc.scalar.activation(
+                out=rms[tt][:], in_=sum_sq[:], func=ACT.Sqrt, scale=1.0 / H, bias=eps[:, 0:1]
+            )
+
+        def reciprocal_rms(tt):
+            rstd[tt] = small.tile([P, 1], F32, name="rstd")
+            nc.vector.reciprocal(rstd[tt][:], rms[tt][:])
+
+        def transpose_tokens(tt):
+            for g in range(H_PASSES):
+                h_t[tt, g] = psum.tile([P, PACK, P], F32, tag="bank", name="h_t")
+                for j in range(PACK):
+                    k0 = K_PASS * g + P * j
+                    nc.tensor.transpose(
+                        h_t[tt, g][:, j, :], h_scaled[tt][:, k0 : k0 + P], ident[:]
+                    )
+
+        def apply_gain(tt):
+            for g in range(H_PASSES):
+                nc.vector.tensor_tensor(
+                    out=n_grouped[:, tt, g, :, :],
+                    in0=h_t[tt, g][:].rearrange("p j t -> p t j"),
+                    in1=gain[:, PACK * g : PACK * (g + 1)].unsqueeze(1).to_broadcast([P, P, PACK]),
+                    op=ALU.mult,
+                )
+
+        def quantise_tokens(tt):
+            nc.vector.quantize_mx(
+                out=n_codes[:, tt].rearrange("p g t -> p (g t)").bitcast(FP8X4),
+                scales=n_scales[:, tt].rearrange("p g t -> p (g t)"),
+                in_=n_grouped[:, tt].rearrange("p g t j -> p (g t j)"),
+            )
+
+        def load_v(m, piece):
+            raw = raw_pool.tile([P, 2, PACK, R], BF16, tag="raw", name="raw_v")
+            nc.sync.dma_start(out=raw[:], in_=v_views[m][:, 2 * piece : 2 * piece + 2, :, :])
+            raw_halves["v", m, piece] = [raw[:, 0], raw[:, 1]]
+
+        def load_u(piece):
+            if piece < U_PIECES:
+                for m in (GATE, UP):
+                    raw = raw_pool.tile([P, PACK, PIECE], BF16, tag="raw", name="raw_u")
+                    nc.sync.dma_start(
+                        out=raw[:], in_=u_views[m][:, :, piece * PIECE : (piece + 1) * PIECE]
+                    )
+                    raw_halves["u", m, piece] = [raw[:, :, 0:HALF], raw[:, :, HALF:PIECE]]
+
+        def regroup(kind, m, piece, halves):
+            key = (kind, m, piece)
+            if key in raw_halves:
+                if key not in grouped:
+                    grouped[key] = grouped_pool.tile(
+                        [P, 2, HALF, PACK], BF16, align_bytes=64, name="grouped"
+                    )
+                for half in halves:
+                    regroup_copy[m](
+                        out=grouped[key][:, half].rearrange("p (c i) j -> p c j i", i=RUN),
+                        in_=raw_halves[key][half].rearrange("p j (c i) -> p c j i", i=RUN),
+                    )
+
+        def quantise_v(m, piece):
+            passes = slice(2 * piece, 2 * piece + 2)
+            nc.vector.quantize_mx(
+                out=v_codes[m][:, passes, :].rearrange("p g r -> p (g r)").bitcast(FP8X4),
+                scales=v_scales[m][:, passes, :].rearrange("p g r -> p (g r)"),
+                in_=grouped["v", m, piece][:].rearrange("p h c j -> p (h c j)"),
+            )
+
+        def quantise_u(m, piece):
+            if piece < U_PIECES:
+                u_codes[m, piece] = u_pool.tile([P, PIECE], U32, align_bytes=64, name="u_codes")
+                u_scales[m, piece] = u_pool.tile([P, PIECE], U8, align_bytes=64, name="u_scales")
+                nc.vector.quantize_mx(
+                    out=u_codes[m, piece][:].bitcast(FP8X4),
+                    scales=u_scales[m, piece][:],
+                    in_=grouped["u", m, piece][:].rearrange("p h c j -> p (h c j)"),
+                )
+
+        def first_product(m, tt):
+            r_t[m, tt] = psum.tile([P, PACK, P], F32, tag="bank", name="r_t")
+            for j in range(PACK):
+                r_cols = slice(P * j, P * (j + 1))
+                for g in range(H_PASSES):
+                    nc.tensor.matmul_mx(
+                        out=r_t[m, tt][:, j, :],
+                        lhsT=v_codes[m][:, g, r_cols].bitcast(FP8X4),
+                        lhsT_scale=v_scales[m][:, g, r_cols],
+                        rhs=n_codes[:, tt, g, :].bitcast(FP8X4),
+                        rhs_scale=n_scales[:, tt, g, :],
+                        start=(g == 0),
+                        stop=(g == H_PASSES - 1),
+                    )
+
+        def round_first_product(m, tt):
+            nc.scalar.copy(
+                out=r_grouped[:, m, tt, :, :], in_=r_t[m, tt][:].rearrange("p j t -> p t j")
+            )
+
+        def second_products(piece):
+            for tt in range(TOKEN_TILES):
+                for b in range(BANKS_PER_PIECE):
+                    cols = slice(b * BANK, (b + 1) * BANK)
+                    for m in (GATE, UP):
+                        banks[m, tt, b] = psum.tile([P, BANK], F32, tag="bank", name="bank")
+                        nc.tensor.matmul_mx(
+                            out=banks[m, tt, b][:],
+                            lhsT=r_codes[:, m, tt, :].bitcast(FP8X4),
+                            lhsT_scale=r_scales[:, m, tt, :],
+                            rhs=u_codes[m, piece][:, cols].bitcast(FP8X4),
+                            rhs_scale=u_scales[m, piece][:, cols],
+                            start=True,
+                            stop=True,
+                        )
+
+        def finish(piece, tt):
+            product[tt] = product_pool.tile([P, PIECE], F32, name="product")
+            for b in range(BANKS_PER_PIECE):
+                gate_act[b] = act_pool.tile([P, BANK], F32, name="gate_act")
+                nc.scalar.activation(out=gate_act[b][:], in_=banks[GATE, tt, b][:], func=ACT.Silu)
+            for b in range(BANKS_PER_PIECE):
+                nc.vector.tensor_tensor(
+                    out=product[tt][:, b * BANK : (b + 1) * BANK],
+                    in0=gate_act[b][:], in1=banks[UP, tt, b][:], op=ALU.mult,
+                )
+            nc.sync.dma_start(
+                out=out_rows[tt * P : (tt + 1) * P, piece * PIECE : (piece + 1) * PIECE],
+                in_=product[tt][:],
+            )
+
+        eps = const.tile([P, 1], F32)
+        nc.vector.memset(eps[:], EPS)
+        warm = const.tile([P, 2], F32)
+        nc.scalar.sqrt(warm[:, 0:1], eps[:])
+        ident = const.tile([P, P], F32)
+        make_identity(nc, ident[:])
+        gain_rows = const.tile([P, P], BF16)
+        nc.vector.memset(gain_rows[:], 0.0)
+
+        load_tokens(0)
+        load_tokens(1)
+        nc.sync.dma_start(out=gain_rows[0 : H // P, :], in_=ln_w.rearrange("(c p) -> c p", p=P))
+        for m in (GATE, UP):
+            for piece in range(V_PIECES):
+                load_v(m, piece)
+        add_residual(0)
+        root_mean_square(0)
+        add_residual(1)
+        root_mean_square(1)
+        gain_rows_f32 = const.tile([P, P], F32)
+        nc.vector.tensor_copy(out=gain_rows_f32[:], in_=gain_rows[:])
+        gain_bank = psum.tile([P, P], F32, tag="bank")
+        nc.tensor.transpose(gain_bank[:], gain_rows_f32[:], ident[:])
+        gain = const.tile([P, H // P], F32)
+        nc.vector.tensor_copy(out=gain[:], in_=gain_bank[:, 0 : H // P])
+        load_u(0)
+        load_u(1)
+        reciprocal_rms(0)
+        nc.vector.tensor_scalar_mul(out=h_scaled[0][:], in0=h[0][:], scalar1=rstd[0][:, 0:1])
+        transpose_tokens(0)
+        regroup("v", GATE, 0, (0, 1))
+        reciprocal_rms(1)
+        nc.scalar.activation(out=h_scaled[1][:], in_=h[1][:], func=ACT.Copy, scale=rstd[1][:, 0:1])
+        nc.scalar.activation(out=warm[:, 1:2], in_=eps[:], func=ACT.Silu)
+        transpose_tokens(1)
+        regroup("v", GATE, 1, (0, 1))
+        regroup("v", UP, 0, (0, 1))
+        apply_gain(0)
+        apply_gain(1)
+        quantise_tokens(0)
+        quantise_tokens(1)
+        quantise_v(GATE, 0)
+        quantise_v(GATE, 1)
+        first_product(GATE, 0)
+        first_product(GATE, 1)
+        regroup("v", UP, 1, (0, 1))
+        load_u(2)
+        load_u(3)
+        quantise_v(UP, 0)
+        regroup("u", GATE, 0, (0, 1))
+        quantise_v(UP, 1)
+        first_product(UP, 0)
+        first_product(UP, 1)
+        round_first_product(GATE, 0)
+        round_first_product(GATE, 1)
+        regroup("u", UP, 0, (0, 1))
+        load_u(4)
+        quantise_u(GATE, 0)
+        regroup("u", GATE, 1, (0, 1))
+        round_first_product(UP, 0)
+        round_first_product(UP, 1)
+        quantise_u(UP, 0)
+        nc.vector.quantize_mx(
+            out=r_codes[:].rearrange("p m a t -> p (m a t)").bitcast(FP8X4),
+            scales=r_scales[:].rearrange("p m a t -> p (m a t)"),
+            in_=r_grouped[:].rearrange("p m a t j -> p (m a t j)"),
+        )
+        regroup("u", UP, 1, (0,))
+
+        for s in range(U_PIECES):
+            load_u(s + LOADS_AHEAD)
+            second_products(s)
+            regroup("u", UP, s + 1, (1,))
+            quantise_u(GATE, s + 1)
+            regroup("u", GATE, s + 2, (0,))
+            finish(s, 0)
+            regroup("u", UP, s + 2, (0,))
+            quantise_u(UP, s + 1)
+            regroup("u", GATE, s + 2, (1,))
+            finish(s, 1)

@@ -30,6 +30,7 @@ U_PIECES = I // PIECE
 RUN = 4
 GATE = 0
 UP = 1
+U_LOAD = 2 * PIECE
 LOADS_AHEAD = 5
 
 FLOPS = 2 * TOKENS * (2 * H * R + 2 * R * I)
@@ -42,7 +43,7 @@ def tile_neuronllamamlp_pa_kernel(
     x_rows = x.flatten_outer_dims()
     res_rows = residual.flatten_outer_dims()
     out_rows = out.flatten_outer_dims()
-    v_views = [w.rearrange("(g j p) r -> p g j r", j=PACK, p=P) for w in (w_gate_v, w_up_v)]
+    v_views = [w.rearrange("(g p j) r -> p g j r", j=PACK, p=P) for w in (w_gate_v, w_up_v)]
     u_views = [w.rearrange("(j p) i -> p j i", p=P) for w in (w_gate_u, w_up_u)]
     regroup_copy = (nc.vector.tensor_copy, nc.scalar.copy)
 
@@ -50,7 +51,7 @@ def tile_neuronllamamlp_pa_kernel(
         const = ctx.enter_context(tc.tile_pool(name="const", bufs=1))
         keep = ctx.enter_context(tc.tile_pool(name="keep", bufs=1))
         small = ctx.enter_context(tc.tile_pool(name="small", bufs=2))
-        raw_pool = ctx.enter_context(tc.tile_pool(name="raw", bufs=12))
+        raw_pool = ctx.enter_context(tc.tile_pool(name="raw", bufs=6))
         grouped_pool = ctx.enter_context(tc.tile_pool(name="grouped", bufs=4))
         u_pool = ctx.enter_context(tc.tile_pool(name="u_codes", bufs=4))
         act_pool = ctx.enter_context(tc.tile_pool(name="gate_act", bufs=3))
@@ -73,27 +74,28 @@ def tile_neuronllamamlp_pa_kernel(
         r_codes = keep.tile([P, 2, TOKEN_TILES, P], U32, align_bytes=64)
         r_scales = keep.tile([P, 2, TOKEN_TILES, P], U8, align_bytes=64)
 
-        x_res, h, h_scaled, rms, rstd, h_t = {}, {}, {}, {}, {}, {}
+        rms, rstd, h_t = {}, {}, {}
         raw_halves, grouped, u_codes, u_scales = {}, {}, {}, {}
         r_t, banks, gate_act, product = {}, {}, {}, {}
 
+        x_res = raw_pool.tile([P, TOKEN_TILES, 2, H], BF16, tag="raw")
+        h = raw_pool.tile([P, TOKEN_TILES, H], F32, tag="raw")
+        h_scaled = raw_pool.tile([P, TOKEN_TILES, H], F32, tag="raw")
+
         def load_tokens(tt):
             rows = slice(tt * P, (tt + 1) * P)
-            x_res[tt] = raw_pool.tile([P, 2, H], BF16, tag="raw", name="x_res")
-            nc.sync.dma_start(out=x_res[tt][:, 0, :], in_=x_rows[rows, :])
-            nc.sync.dma_start(out=x_res[tt][:, 1, :], in_=res_rows[rows, :])
+            nc.sync.dma_start(out=x_res[:, tt, 0, :], in_=x_rows[rows, :])
+            nc.sync.dma_start(out=x_res[:, tt, 1, :], in_=res_rows[rows, :])
 
         def add_residual(tt):
-            h[tt] = raw_pool.tile([P, H], F32, tag="raw", name="h")
             nc.vector.tensor_tensor(
-                out=h[tt][:], in0=x_res[tt][:, 0, :], in1=x_res[tt][:, 1, :], op=ALU.add
+                out=h[:, tt, :], in0=x_res[:, tt, 0, :], in1=x_res[:, tt, 1, :], op=ALU.add
             )
 
         def root_mean_square(tt):
-            h_scaled[tt] = raw_pool.tile([P, H], F32, tag="raw", name="h_scaled")
             sum_sq = small.tile([P, 1], F32, name="sum_sq")
             nc.scalar.activation(
-                out=h_scaled[tt][:], in_=h[tt][:], func=ACT.Square, accum_out=sum_sq[:]
+                out=h_scaled[:, tt, :], in_=h[:, tt, :], func=ACT.Square, accum_out=sum_sq[:]
             )
             rms[tt] = small.tile([P, 1], F32, name="rms")
             nc.scalar.activation(
@@ -104,13 +106,19 @@ def tile_neuronllamamlp_pa_kernel(
             rstd[tt] = small.tile([P, 1], F32, name="rstd")
             nc.vector.reciprocal(rstd[tt][:], rms[tt][:])
 
+        def scaled_views(tt):
+            return (
+                h_scaled[:, tt, :].rearrange("t (g j p) -> t g p j", g=H_PASSES, j=PACK),
+                h[:, tt, :].rearrange("t (g p j) -> t g p j", g=H_PASSES, j=PACK),
+            )
+
         def transpose_tokens(tt):
             for g in range(H_PASSES):
                 h_t[tt, g] = psum.tile([P, PACK, P], F32, tag="bank", name="h_t")
                 for j in range(PACK):
-                    k0 = K_PASS * g + P * j
+                    plane = P * (PACK * g + j)
                     nc.tensor.transpose(
-                        h_t[tt, g][:, j, :], h_scaled[tt][:, k0 : k0 + P], ident[:]
+                        h_t[tt, g][:, j, :], h_scaled[:, tt, plane : plane + P], ident[:]
                     )
 
         def apply_gain(tt):
@@ -129,19 +137,26 @@ def tile_neuronllamamlp_pa_kernel(
                 in_=n_grouped[:, tt].rearrange("p g t j -> p (g t j)"),
             )
 
-        def load_v(m, piece):
-            raw = raw_pool.tile([P, 2, PACK, R], BF16, tag="raw", name="raw_v")
-            nc.sync.dma_start(out=raw[:], in_=v_views[m][:, 2 * piece : 2 * piece + 2, :, :])
-            raw_halves["v", m, piece] = [raw[:, 0], raw[:, 1]]
+        def load_v(m):
+            raw = raw_pool.tile([P, H_PASSES, PACK, R], BF16, tag="raw", name="raw_v")
+            for piece in range(V_PIECES):
+                passes = slice(2 * piece, 2 * piece + 2)
+                nc.sync.dma_start(out=raw[:, passes], in_=v_views[m][:, passes, :, :])
+                raw_halves["v", m, piece] = [raw[:, 2 * piece], raw[:, 2 * piece + 1]]
 
-        def load_u(piece):
-            if piece < U_PIECES:
+        def load_u(load):
+            first = load * U_LOAD
+            width = min(U_LOAD, I - first)
+            if width > 0:
                 for m in (GATE, UP):
-                    raw = raw_pool.tile([P, PACK, PIECE], BF16, tag="raw", name="raw_u")
+                    raw = raw_pool.tile([P, PACK, U_LOAD], BF16, tag="raw", name="raw_u")
                     nc.sync.dma_start(
-                        out=raw[:], in_=u_views[m][:, :, piece * PIECE : (piece + 1) * PIECE]
+                        out=raw[:, :, 0:width], in_=u_views[m][:, :, first : first + width]
                     )
-                    raw_halves["u", m, piece] = [raw[:, :, 0:HALF], raw[:, :, HALF:PIECE]]
+                    for c0 in range(0, width, PIECE):
+                        raw_halves["u", m, (first + c0) // PIECE] = [
+                            raw[:, :, c0 : c0 + HALF], raw[:, :, c0 + HALF : c0 + PIECE]
+                        ]
 
         def regroup(kind, m, piece, halves):
             key = (kind, m, piece)
@@ -231,33 +246,29 @@ def tile_neuronllamamlp_pa_kernel(
         nc.scalar.sqrt(warm[:, 0:1], eps[:])
         ident = const.tile([P, P], F32)
         make_identity(nc, ident[:])
-        gain_rows = const.tile([P, P], BF16)
-        nc.vector.memset(gain_rows[:], 0.0)
 
         load_tokens(0)
         load_tokens(1)
-        nc.sync.dma_start(out=gain_rows[0 : H // P, :], in_=ln_w.rearrange("(c p) -> c p", p=P))
-        for m in (GATE, UP):
-            for piece in range(V_PIECES):
-                load_v(m, piece)
+        gain = const.tile([P, H_PASSES * PACK], BF16)
+        nc.sync.dma_start(
+            out=gain[:].rearrange("p (g j) -> p g j", j=PACK),
+            in_=ln_w.rearrange("(g p j) -> p g j", p=P, j=PACK),
+        )
+        load_v(GATE)
+        load_v(UP)
         add_residual(0)
         root_mean_square(0)
         add_residual(1)
         root_mean_square(1)
-        gain_rows_f32 = const.tile([P, P], F32)
-        nc.vector.tensor_copy(out=gain_rows_f32[:], in_=gain_rows[:])
-        gain_bank = psum.tile([P, P], F32, tag="bank")
-        nc.tensor.transpose(gain_bank[:], gain_rows_f32[:], ident[:])
-        gain = const.tile([P, H // P], F32)
-        nc.vector.tensor_copy(out=gain[:], in_=gain_bank[:, 0 : H // P])
         load_u(0)
-        load_u(1)
         reciprocal_rms(0)
-        nc.vector.tensor_scalar_mul(out=h_scaled[0][:], in0=h[0][:], scalar1=rstd[0][:, 0:1])
+        planes, in_order = scaled_views(0)
+        nc.vector.tensor_scalar_mul(out=planes, in0=in_order, scalar1=rstd[0][:, 0:1])
         transpose_tokens(0)
         regroup("v", GATE, 0, (0, 1))
         reciprocal_rms(1)
-        nc.scalar.activation(out=h_scaled[1][:], in_=h[1][:], func=ACT.Copy, scale=rstd[1][:, 0:1])
+        planes, in_order = scaled_views(1)
+        nc.scalar.activation(out=planes, in_=in_order, func=ACT.Copy, scale=rstd[1][:, 0:1])
         nc.scalar.activation(out=warm[:, 1:2], in_=eps[:], func=ACT.Silu)
         transpose_tokens(1)
         regroup("v", GATE, 1, (0, 1))
@@ -271,8 +282,8 @@ def tile_neuronllamamlp_pa_kernel(
         first_product(GATE, 0)
         first_product(GATE, 1)
         regroup("v", UP, 1, (0, 1))
+        load_u(1)
         load_u(2)
-        load_u(3)
         quantise_v(UP, 0)
         regroup("u", GATE, 0, (0, 1))
         quantise_v(UP, 1)
@@ -281,7 +292,6 @@ def tile_neuronllamamlp_pa_kernel(
         round_first_product(GATE, 0)
         round_first_product(GATE, 1)
         regroup("u", UP, 0, (0, 1))
-        load_u(4)
         quantise_u(GATE, 0)
         regroup("u", GATE, 1, (0, 1))
         round_first_product(UP, 0)
@@ -295,7 +305,8 @@ def tile_neuronllamamlp_pa_kernel(
         regroup("u", UP, 1, (0,))
 
         for s in range(U_PIECES):
-            load_u(s + LOADS_AHEAD)
+            if (s + LOADS_AHEAD) % 2 == 0:
+                load_u((s + LOADS_AHEAD) // 2)
             second_products(s)
             regroup("u", UP, s + 1, (1,))
             quantise_u(GATE, s + 1)

@@ -18,6 +18,7 @@ TOKENS = 256
 TOKEN_TILES = TOKENS // P
 H = 2048
 H_PASSES = H // K_PASS
+H_HALVES = (slice(0, H // 2), slice(H // 2, H))
 R = 512
 I = 7168
 EPS = 1e-05
@@ -30,8 +31,16 @@ U_PIECES = I // PIECE
 RUN = 4
 GATE = 0
 UP = 1
-U_LOAD = 2 * PIECE
+GATE_VECTOR_COLS = 704
 LOADS_AHEAD = 5
+RAW_SLOTS = 10
+GROUPED_SLOTS = 4
+UP_FIRST_HALF_SLOTS = 2
+UP_SECOND_HALF_SLOTS = 1
+CODE_SLOTS = 4
+ACT_SLOTS = 6
+PRODUCT_SLOTS = 8
+PSUM_BANKS = 8
 
 FLOPS = 2 * TOKENS * (2 * H * R + 2 * R * I)
 
@@ -43,82 +52,86 @@ def tile_neuronllamamlp_pa_kernel(
     x_rows = x.flatten_outer_dims()
     res_rows = residual.flatten_outer_dims()
     out_rows = out.flatten_outer_dims()
-    v_views = [w.rearrange("(g p j) r -> p g j r", j=PACK, p=P) for w in (w_gate_v, w_up_v)]
+    v_views = [w.rearrange("(g j p) r -> p g j r", j=PACK, p=P) for w in (w_gate_v, w_up_v)]
     u_views = [w.rearrange("(j p) i -> p j i", p=P) for w in (w_gate_u, w_up_u)]
-    regroup_copy = (nc.vector.tensor_copy, nc.scalar.copy)
 
     with ExitStack() as ctx:
         const = ctx.enter_context(tc.tile_pool(name="const", bufs=1))
         keep = ctx.enter_context(tc.tile_pool(name="keep", bufs=1))
-        small = ctx.enter_context(tc.tile_pool(name="small", bufs=2))
-        raw_pool = ctx.enter_context(tc.tile_pool(name="raw", bufs=6))
-        grouped_pool = ctx.enter_context(tc.tile_pool(name="grouped", bufs=4))
-        u_pool = ctx.enter_context(tc.tile_pool(name="u_codes", bufs=4))
-        act_pool = ctx.enter_context(tc.tile_pool(name="gate_act", bufs=3))
-        product_pool = ctx.enter_context(tc.tile_pool(name="product", bufs=4))
-        psum = ctx.enter_context(tc.psum_pool(name="psum", bufs=8))
+        small = ctx.enter_context(tc.tile_pool(name="small", bufs=TOKEN_TILES))
+        raw_pool = ctx.enter_context(tc.tile_pool(name="raw", bufs=RAW_SLOTS))
+        grouped_pool = ctx.enter_context(tc.tile_pool(name="grouped", bufs=GROUPED_SLOTS))
+        up_first_pool = ctx.enter_context(tc.tile_pool(name="up_a", bufs=UP_FIRST_HALF_SLOTS))
+        up_second_pool = ctx.enter_context(tc.tile_pool(name="up_b", bufs=UP_SECOND_HALF_SLOTS))
+        u_pool = ctx.enter_context(tc.tile_pool(name="u_codes", bufs=CODE_SLOTS))
+        act_pool = ctx.enter_context(tc.tile_pool(name="gate_act", bufs=ACT_SLOTS))
+        product_pool = ctx.enter_context(tc.tile_pool(name="product", bufs=PRODUCT_SLOTS))
+        psum = ctx.enter_context(tc.psum_pool(name="psum", bufs=PSUM_BANKS))
         ctx.enter_context(tc.manual_schedule())
+
 
         n_grouped = keep.tile([P, TOKEN_TILES, H_PASSES, P, PACK], BF16, align_bytes=64)
         n_codes = keep.tile([P, TOKEN_TILES, H_PASSES, P], U32, align_bytes=64)
         n_scales = keep.tile([P, TOKEN_TILES, H_PASSES, P], U8, align_bytes=64)
         v_codes = [
-            keep.tile([P, H_PASSES, R], U32, align_bytes=64, name="v_codes%d" % m)
+            keep.tile([P, V_PIECES * PIECE], U32, align_bytes=64, name="v_codes%d" % m)
             for m in (GATE, UP)
         ]
         v_scales = [
-            keep.tile([P, H_PASSES, R], U8, align_bytes=64, name="v_scales%d" % m)
+            keep.tile([P, V_PIECES * PIECE], U8, align_bytes=64, name="v_scales%d" % m)
             for m in (GATE, UP)
         ]
         r_grouped = keep.tile([P, 2, TOKEN_TILES, P, PACK], BF16, align_bytes=64)
         r_codes = keep.tile([P, 2, TOKEN_TILES, P], U32, align_bytes=64)
         r_scales = keep.tile([P, 2, TOKEN_TILES, P], U8, align_bytes=64)
 
-        rms, rstd, h_t = {}, {}, {}
-        raw_halves, grouped, u_codes, u_scales = {}, {}, {}, {}
-        r_t, banks, gate_act, product = {}, {}, {}, {}
-
-        x_res = raw_pool.tile([P, TOKEN_TILES, 2, H], BF16, tag="raw")
-        h = raw_pool.tile([P, TOKEN_TILES, H], F32, tag="raw")
-        h_scaled = raw_pool.tile([P, TOKEN_TILES, H], F32, tag="raw")
+        x_res, h, h_scaled, sum_sq, rms, rstd, h_t = {}, {}, {}, {}, {}, {}, {}
+        raw, grouped_parts, codes, scales = {}, {}, {}, {}
+        r_t, banks, gate_act = {}, {}, {}
 
         def load_tokens(tt):
             rows = slice(tt * P, (tt + 1) * P)
-            nc.sync.dma_start(out=x_res[:, tt, 0, :], in_=x_rows[rows, :])
-            nc.sync.dma_start(out=x_res[:, tt, 1, :], in_=res_rows[rows, :])
+            x_res[tt] = raw_pool.tile([P, 2, H], BF16, tag="raw", name="x_res")
+            h[tt] = raw_pool.tile([P, H], F32, tag="raw", name="h")
+            h_scaled[tt] = raw_pool.tile([P, H], F32, tag="raw", name="h_scaled")
+            sum_sq[tt] = small.tile([P, 2], F32, name="sum_sq")
+            for cols in H_HALVES:
+                nc.sync.dma_start(out=x_res[tt][:, 0, cols], in_=x_rows[rows, cols])
+                nc.sync.dma_start(out=x_res[tt][:, 1, cols], in_=res_rows[rows, cols])
 
-        def add_residual(tt):
+        def add_and_square(tt, half):
+            cols = H_HALVES[half]
             nc.vector.tensor_tensor(
-                out=h[:, tt, :], in0=x_res[:, tt, 0, :], in1=x_res[:, tt, 1, :], op=ALU.add
+                out=h[tt][:, cols], in0=x_res[tt][:, 0, cols], in1=x_res[tt][:, 1, cols], op=ALU.add
+            )
+            nc.scalar.activation(
+                out=h_scaled[tt][:, cols], in_=h[tt][:, cols], func=ACT.Square,
+                accum_out=sum_sq[tt][:, half : half + 1],
             )
 
         def root_mean_square(tt):
-            sum_sq = small.tile([P, 1], F32, name="sum_sq")
+            first_mean = small.tile([P, 1], F32, name="first_mean")
             nc.scalar.activation(
-                out=h_scaled[:, tt, :], in_=h[:, tt, :], func=ACT.Square, accum_out=sum_sq[:]
+                out=first_mean[:], in_=sum_sq[tt][:, 0:1], func=ACT.Identity,
+                scale=1.0 / H, bias=eps[:, 0:1],
             )
             rms[tt] = small.tile([P, 1], F32, name="rms")
             nc.scalar.activation(
-                out=rms[tt][:], in_=sum_sq[:], func=ACT.Sqrt, scale=1.0 / H, bias=eps[:, 0:1]
+                out=rms[tt][:], in_=sum_sq[tt][:, 1:2], func=ACT.Sqrt,
+                scale=1.0 / H, bias=first_mean[:, 0:1],
             )
 
         def reciprocal_rms(tt):
             rstd[tt] = small.tile([P, 1], F32, name="rstd")
             nc.vector.reciprocal(rstd[tt][:], rms[tt][:])
 
-        def scaled_views(tt):
-            return (
-                h_scaled[:, tt, :].rearrange("t (g j p) -> t g p j", g=H_PASSES, j=PACK),
-                h[:, tt, :].rearrange("t (g p j) -> t g p j", g=H_PASSES, j=PACK),
-            )
-
         def transpose_tokens(tt):
             for g in range(H_PASSES):
                 h_t[tt, g] = psum.tile([P, PACK, P], F32, tag="bank", name="h_t")
                 for j in range(PACK):
-                    plane = P * (PACK * g + j)
+                    k0 = K_PASS * g + P * j
                     nc.tensor.transpose(
-                        h_t[tt, g][:, j, :], h_scaled[:, tt, plane : plane + P], ident[:]
+                        h_t[tt, g][:, j, :], h_scaled[tt][:, k0 : k0 + P], ident[:]
                     )
 
         def apply_gain(tt):
@@ -137,67 +150,81 @@ def tile_neuronllamamlp_pa_kernel(
                 in_=n_grouped[:, tt].rearrange("p g t j -> p (g t j)"),
             )
 
-        def load_v(m):
-            raw = raw_pool.tile([P, H_PASSES, PACK, R], BF16, tag="raw", name="raw_v")
-            for piece in range(V_PIECES):
-                passes = slice(2 * piece, 2 * piece + 2)
-                nc.sync.dma_start(out=raw[:, passes], in_=v_views[m][:, passes, :, :])
-                raw_halves["v", m, piece] = [raw[:, 2 * piece], raw[:, 2 * piece + 1]]
+        def load_v(m, piece):
+            key = ("v", m, piece)
+            raw[key] = raw_pool.tile([P, PACK, PIECE], BF16, tag="raw", name="raw_v")
+            for half in range(2):
+                nc.sync.dma_start(
+                    out=raw[key][:, :, half * R : (half + 1) * R],
+                    in_=v_views[m][:, 2 * piece + half, :, :],
+                )
+            codes[key] = v_codes[m][:, piece * PIECE : (piece + 1) * PIECE]
+            scales[key] = v_scales[m][:, piece * PIECE : (piece + 1) * PIECE]
 
-        def load_u(load):
-            first = load * U_LOAD
-            width = min(U_LOAD, I - first)
-            if width > 0:
+        def load_u(piece):
+            if piece < U_PIECES:
                 for m in (GATE, UP):
-                    raw = raw_pool.tile([P, PACK, U_LOAD], BF16, tag="raw", name="raw_u")
+                    key = ("u", m, piece)
+                    raw[key] = raw_pool.tile([P, PACK, PIECE], BF16, tag="raw", name="raw_u")
                     nc.sync.dma_start(
-                        out=raw[:, :, 0:width], in_=u_views[m][:, :, first : first + width]
-                    )
-                    for c0 in range(0, width, PIECE):
-                        raw_halves["u", m, (first + c0) // PIECE] = [
-                            raw[:, :, c0 : c0 + HALF], raw[:, :, c0 + HALF : c0 + PIECE]
-                        ]
-
-        def regroup(kind, m, piece, halves):
-            key = (kind, m, piece)
-            if key in raw_halves:
-                if key not in grouped:
-                    grouped[key] = grouped_pool.tile(
-                        [P, 2, HALF, PACK], BF16, align_bytes=64, name="grouped"
-                    )
-                for half in halves:
-                    regroup_copy[m](
-                        out=grouped[key][:, half].rearrange("p (c i) j -> p c j i", i=RUN),
-                        in_=raw_halves[key][half].rearrange("p j (c i) -> p c j i", i=RUN),
+                        out=raw[key][:], in_=u_views[m][:, :, piece * PIECE : (piece + 1) * PIECE]
                     )
 
-        def quantise_v(m, piece):
-            passes = slice(2 * piece, 2 * piece + 2)
-            nc.vector.quantize_mx(
-                out=v_codes[m][:, passes, :].rearrange("p g r -> p (g r)").bitcast(FP8X4),
-                scales=v_scales[m][:, passes, :].rearrange("p g r -> p (g r)"),
-                in_=grouped["v", m, piece][:].rearrange("p h c j -> p (h c j)"),
+        def one_grouped_part(key):
+            whole = grouped_pool.tile([P, PIECE, PACK], BF16, align_bytes=64, name="grouped")
+            grouped_parts[key] = [(0, PIECE, whole)]
+
+        def two_grouped_parts(key):
+            first = up_first_pool.tile([P, HALF, PACK], BF16, align_bytes=64, name="up_first")
+            second = up_second_pool.tile([P, HALF, PACK], BF16, align_bytes=64, name="up_second")
+            grouped_parts[key] = [(0, HALF, first), (HALF, PIECE, second)]
+
+        def grouped_columns(key, lo, hi):
+            views = [
+                part[:, lo - start : hi - start, :]
+                for start, end, part in grouped_parts[key]
+                if start <= lo and hi <= end
+            ]
+            return views[0]
+
+        def regroup(copy, key, lo, hi):
+            copy(
+                out=grouped_columns(key, lo, hi).rearrange("p (c i) j -> p c j i", i=RUN),
+                in_=raw[key][:, :, lo:hi].rearrange("p j (c i) -> p c j i", i=RUN),
             )
 
-        def quantise_u(m, piece):
-            if piece < U_PIECES:
-                u_codes[m, piece] = u_pool.tile([P, PIECE], U32, align_bytes=64, name="u_codes")
-                u_scales[m, piece] = u_pool.tile([P, PIECE], U8, align_bytes=64, name="u_scales")
+        def regroup_on_gpsimd(key, lo, hi):
+            nc.gpsimd.tensor_scalar(
+                out=grouped_columns(key, lo, hi),
+                in0=raw[key][:, :, lo:hi].rearrange("p j c -> p c j"),
+                scalar1=1.0, scalar2=0.0, op0=ALU.mult, op1=ALU.add,
+            )
+
+        def regroup_piece(copy, key):
+            one_grouped_part(key)
+            regroup(copy, key, 0, HALF)
+            regroup(copy, key, HALF, PIECE)
+
+        def quantise_piece(key):
+            if key not in codes:
+                codes[key] = u_pool.tile([P, PIECE], U32, align_bytes=64, name="u_codes")
+                scales[key] = u_pool.tile([P, PIECE], U8, align_bytes=64, name="u_scales")
+            for start, end, part in grouped_parts[key]:
                 nc.vector.quantize_mx(
-                    out=u_codes[m, piece][:].bitcast(FP8X4),
-                    scales=u_scales[m, piece][:],
-                    in_=grouped["u", m, piece][:].rearrange("p h c j -> p (h c j)"),
+                    out=codes[key][:, start:end].bitcast(FP8X4),
+                    scales=scales[key][:, start:end],
+                    in_=part[:].rearrange("p c j -> p (c j)"),
                 )
 
         def first_product(m, tt):
             r_t[m, tt] = psum.tile([P, PACK, P], F32, tag="bank", name="r_t")
             for j in range(PACK):
-                r_cols = slice(P * j, P * (j + 1))
                 for g in range(H_PASSES):
+                    r_cols = slice(R * g + P * j, R * g + P * (j + 1))
                     nc.tensor.matmul_mx(
                         out=r_t[m, tt][:, j, :],
-                        lhsT=v_codes[m][:, g, r_cols].bitcast(FP8X4),
-                        lhsT_scale=v_scales[m][:, g, r_cols],
+                        lhsT=v_codes[m][:, r_cols].bitcast(FP8X4),
+                        lhsT_scale=v_scales[m][:, r_cols],
                         rhs=n_codes[:, tt, g, :].bitcast(FP8X4),
                         rhs_scale=n_scales[:, tt, g, :],
                         start=(g == 0),
@@ -210,35 +237,41 @@ def tile_neuronllamamlp_pa_kernel(
             )
 
         def second_products(piece):
-            for tt in range(TOKEN_TILES):
-                for b in range(BANKS_PER_PIECE):
-                    cols = slice(b * BANK, (b + 1) * BANK)
-                    for m in (GATE, UP):
+            for m in (GATE, UP):
+                for tt in range(TOKEN_TILES):
+                    for b in range(BANKS_PER_PIECE):
+                        cols = slice(b * BANK, (b + 1) * BANK)
                         banks[m, tt, b] = psum.tile([P, BANK], F32, tag="bank", name="bank")
                         nc.tensor.matmul_mx(
                             out=banks[m, tt, b][:],
                             lhsT=r_codes[:, m, tt, :].bitcast(FP8X4),
                             lhsT_scale=r_scales[:, m, tt, :],
-                            rhs=u_codes[m, piece][:, cols].bitcast(FP8X4),
-                            rhs_scale=u_scales[m, piece][:, cols],
+                            rhs=codes["u", m, piece][:, cols].bitcast(FP8X4),
+                            rhs_scale=scales["u", m, piece][:, cols],
                             start=True,
                             stop=True,
                         )
 
-        def finish(piece, tt):
-            product[tt] = product_pool.tile([P, PIECE], F32, name="product")
-            for b in range(BANKS_PER_PIECE):
-                gate_act[b] = act_pool.tile([P, BANK], F32, name="gate_act")
-                nc.scalar.activation(out=gate_act[b][:], in_=banks[GATE, tt, b][:], func=ACT.Silu)
-            for b in range(BANKS_PER_PIECE):
-                nc.vector.tensor_tensor(
-                    out=product[tt][:, b * BANK : (b + 1) * BANK],
-                    in0=gate_act[b][:], in1=banks[UP, tt, b][:], op=ALU.mult,
+        def silu_of_gate():
+            for tt in range(TOKEN_TILES):
+                for b in range(BANKS_PER_PIECE):
+                    gate_act[tt, b] = act_pool.tile([P, BANK], F32, name="gate_act")
+                    nc.scalar.activation(
+                        out=gate_act[tt, b][:], in_=banks[GATE, tt, b][:], func=ACT.Silu
+                    )
+
+        def multiply_and_store(piece):
+            for tt in range(TOKEN_TILES):
+                product = product_pool.tile([P, PIECE], F32, name="product")
+                for b in range(BANKS_PER_PIECE):
+                    nc.vector.tensor_tensor(
+                        out=product[:, b * BANK : (b + 1) * BANK],
+                        in0=gate_act[tt, b][:], in1=banks[UP, tt, b][:], op=ALU.mult,
+                    )
+                nc.sync.dma_start(
+                    out=out_rows[tt * P : (tt + 1) * P, piece * PIECE : (piece + 1) * PIECE],
+                    in_=product[:],
                 )
-            nc.sync.dma_start(
-                out=out_rows[tt * P : (tt + 1) * P, piece * PIECE : (piece + 1) * PIECE],
-                in_=product[tt][:],
-            )
 
         eps = const.tile([P, 1], F32)
         nc.vector.memset(eps[:], EPS)
@@ -246,73 +279,88 @@ def tile_neuronllamamlp_pa_kernel(
         nc.scalar.sqrt(warm[:, 0:1], eps[:])
         ident = const.tile([P, P], F32)
         make_identity(nc, ident[:])
+        gain_rows = const.tile([P, P], BF16)
+        nc.vector.memset(gain_rows[:], 0.0)
 
+        on_vector = nc.vector.tensor_copy
+        on_scalar = nc.scalar.copy
         load_tokens(0)
         load_tokens(1)
-        gain = const.tile([P, H_PASSES * PACK], BF16)
-        nc.sync.dma_start(
-            out=gain[:].rearrange("p (g j) -> p g j", j=PACK),
-            in_=ln_w.rearrange("(g p j) -> p g j", p=P, j=PACK),
-        )
-        load_v(GATE)
-        load_v(UP)
-        add_residual(0)
-        root_mean_square(0)
-        add_residual(1)
-        root_mean_square(1)
+        nc.sync.dma_start(out=gain_rows[0 : H // P, :], in_=ln_w.rearrange("(c p) -> c p", p=P))
+        for m in (GATE, UP):
+            for piece in range(V_PIECES):
+                load_v(m, piece)
+        for tt in range(TOKEN_TILES):
+            add_and_square(tt, 0)
+            add_and_square(tt, 1)
+            root_mean_square(tt)
+        gain_rows_f32 = const.tile([P, P], F32)
+        nc.vector.tensor_copy(out=gain_rows_f32[:], in_=gain_rows[:])
+        gain_bank = psum.tile([P, P], F32, tag="bank")
+        nc.tensor.transpose(gain_bank[:], gain_rows_f32[:], ident[:])
+        gain = const.tile([P, H // P], F32)
+        nc.vector.tensor_copy(out=gain[:], in_=gain_bank[:, 0 : H // P])
         load_u(0)
+        load_u(1)
         reciprocal_rms(0)
-        planes, in_order = scaled_views(0)
-        nc.vector.tensor_scalar_mul(out=planes, in0=in_order, scalar1=rstd[0][:, 0:1])
+        nc.vector.tensor_scalar_mul(out=h_scaled[0][:], in0=h[0][:], scalar1=rstd[0][:, 0:1])
         transpose_tokens(0)
-        regroup("v", GATE, 0, (0, 1))
+        regroup_piece(on_vector, ("v", GATE, 0))
         reciprocal_rms(1)
-        planes, in_order = scaled_views(1)
-        nc.scalar.activation(out=planes, in_=in_order, func=ACT.Copy, scale=rstd[1][:, 0:1])
+        nc.scalar.activation(out=h_scaled[1][:], in_=h[1][:], func=ACT.Copy, scale=rstd[1][:, 0:1])
         nc.scalar.activation(out=warm[:, 1:2], in_=eps[:], func=ACT.Silu)
         transpose_tokens(1)
-        regroup("v", GATE, 1, (0, 1))
-        regroup("v", UP, 0, (0, 1))
+        regroup_piece(on_vector, ("v", GATE, 1))
+        regroup_piece(on_scalar, ("v", UP, 0))
         apply_gain(0)
         apply_gain(1)
         quantise_tokens(0)
         quantise_tokens(1)
-        quantise_v(GATE, 0)
-        quantise_v(GATE, 1)
+        quantise_piece(("v", GATE, 0))
+        quantise_piece(("v", GATE, 1))
         first_product(GATE, 0)
         first_product(GATE, 1)
-        regroup("v", UP, 1, (0, 1))
-        load_u(1)
+        regroup_piece(on_scalar, ("v", UP, 1))
         load_u(2)
-        quantise_v(UP, 0)
-        regroup("u", GATE, 0, (0, 1))
-        quantise_v(UP, 1)
+        load_u(3)
+        quantise_piece(("v", UP, 0))
+        regroup_piece(on_vector, ("u", GATE, 0))
+        quantise_piece(("v", UP, 1))
         first_product(UP, 0)
         first_product(UP, 1)
         round_first_product(GATE, 0)
         round_first_product(GATE, 1)
-        regroup("u", UP, 0, (0, 1))
-        quantise_u(GATE, 0)
-        regroup("u", GATE, 1, (0, 1))
+        two_grouped_parts(("u", UP, 0))
+        regroup(on_scalar, ("u", UP, 0), 0, HALF)
+        regroup(on_scalar, ("u", UP, 0), HALF, PIECE)
+        load_u(4)
+        quantise_piece(("u", GATE, 0))
+        regroup_piece(on_vector, ("u", GATE, 1))
         round_first_product(UP, 0)
         round_first_product(UP, 1)
-        quantise_u(UP, 0)
+        quantise_piece(("u", UP, 0))
         nc.vector.quantize_mx(
             out=r_codes[:].rearrange("p m a t -> p (m a t)").bitcast(FP8X4),
             scales=r_scales[:].rearrange("p m a t -> p (m a t)"),
             in_=r_grouped[:].rearrange("p m a t j -> p (m a t j)"),
         )
-        regroup("u", UP, 1, (0,))
+        two_grouped_parts(("u", UP, 1))
+        regroup(on_scalar, ("u", UP, 1), 0, HALF)
+        regroup(on_scalar, ("u", UP, 1), HALF, PIECE)
 
         for s in range(U_PIECES):
-            if (s + LOADS_AHEAD) % 2 == 0:
-                load_u((s + LOADS_AHEAD) // 2)
+            load_u(s + LOADS_AHEAD)
             second_products(s)
-            regroup("u", UP, s + 1, (1,))
-            quantise_u(GATE, s + 1)
-            regroup("u", GATE, s + 2, (0,))
-            finish(s, 0)
-            regroup("u", UP, s + 2, (0,))
-            quantise_u(UP, s + 1)
-            regroup("u", GATE, s + 2, (1,))
-            finish(s, 1)
+            silu_of_gate()
+            if s + 2 < U_PIECES:
+                one_grouped_part(("u", GATE, s + 2))
+                regroup(on_vector, ("u", GATE, s + 2), 0, GATE_VECTOR_COLS)
+                regroup(on_scalar, ("u", GATE, s + 2), GATE_VECTOR_COLS, PIECE)
+            if s + 1 < U_PIECES:
+                quantise_piece(("u", GATE, s + 1))
+                quantise_piece(("u", UP, s + 1))
+            if s + 2 < U_PIECES:
+                two_grouped_parts(("u", UP, s + 2))
+                regroup(on_scalar, ("u", UP, s + 2), 0, HALF)
+                regroup_on_gpsimd(("u", UP, s + 2), HALF, PIECE)
+            multiply_and_store(s)

from contextlib import ExitStack

import concourse.mybir as mybir
from concourse.masks import make_identity

F32 = mybir.dt.float32
BF16 = mybir.dt.bfloat16
U32 = mybir.dt.uint32
U8 = mybir.dt.uint8
FP8X4 = mybir.dt.float8_e4m3fn_x4
ACT = mybir.ActivationFunctionType
ALU = mybir.AluOpType

P = 128
PACK = 4
K_PASS = P * PACK
TOKENS = 256
TOKEN_TILES = TOKENS // P
H = 2048
H_PASSES = H // K_PASS
H_HALVES = (slice(0, H // 2), slice(H // 2, H))
R = 512
I = 7168
EPS = 1e-05
BANK = 512
HALF = 512
PIECE = 2 * HALF
BANKS_PER_PIECE = PIECE // BANK
V_PIECES = H_PASSES * R // PIECE
U_PIECES = I // PIECE
RUN = 4
GATE = 0
UP = 1
GATE_VECTOR_COLS = 704
LOADS_AHEAD = 5
RAW_SLOTS = 10
GROUPED_SLOTS = 4
UP_FIRST_HALF_SLOTS = 2
UP_SECOND_HALF_SLOTS = 1
CODE_SLOTS = 4
ACT_SLOTS = 6
PRODUCT_SLOTS = 8
PSUM_BANKS = 8

FLOPS = 2 * TOKENS * (2 * H * R + 2 * R * I)


def tile_neuronllamamlp_pa_kernel(
    tc, x, residual, ln_w, w_gate_v, w_gate_u, w_up_v, w_up_u, out
):
    nc = tc.nc
    x_rows = x.flatten_outer_dims()
    res_rows = residual.flatten_outer_dims()
    out_rows = out.flatten_outer_dims()
    v_views = [w.rearrange("(g j p) r -> p g j r", j=PACK, p=P) for w in (w_gate_v, w_up_v)]
    u_views = [w.rearrange("(j p) i -> p j i", p=P) for w in (w_gate_u, w_up_u)]

    with ExitStack() as ctx:
        const = ctx.enter_context(tc.tile_pool(name="const", bufs=1))
        keep = ctx.enter_context(tc.tile_pool(name="keep", bufs=1))
        small = ctx.enter_context(tc.tile_pool(name="small", bufs=TOKEN_TILES))
        raw_pool = ctx.enter_context(tc.tile_pool(name="raw", bufs=RAW_SLOTS))
        grouped_pool = ctx.enter_context(tc.tile_pool(name="grouped", bufs=GROUPED_SLOTS))
        up_first_pool = ctx.enter_context(tc.tile_pool(name="up_a", bufs=UP_FIRST_HALF_SLOTS))
        up_second_pool = ctx.enter_context(tc.tile_pool(name="up_b", bufs=UP_SECOND_HALF_SLOTS))
        u_pool = ctx.enter_context(tc.tile_pool(name="u_codes", bufs=CODE_SLOTS))
        act_pool = ctx.enter_context(tc.tile_pool(name="gate_act", bufs=ACT_SLOTS))
        product_pool = ctx.enter_context(tc.tile_pool(name="product", bufs=PRODUCT_SLOTS))
        psum = ctx.enter_context(tc.psum_pool(name="psum", bufs=PSUM_BANKS))
        ctx.enter_context(tc.manual_schedule())


        n_grouped = keep.tile([P, TOKEN_TILES, H_PASSES, P, PACK], BF16, align_bytes=64)
        n_codes = keep.tile([P, TOKEN_TILES, H_PASSES, P], U32, align_bytes=64)
        n_scales = keep.tile([P, TOKEN_TILES, H_PASSES, P], U8, align_bytes=64)
        v_codes = [
            keep.tile([P, V_PIECES * PIECE], U32, align_bytes=64, name="v_codes%d" % m)
            for m in (GATE, UP)
        ]
        v_scales = [
            keep.tile([P, V_PIECES * PIECE], U8, align_bytes=64, name="v_scales%d" % m)
            for m in (GATE, UP)
        ]
        r_grouped = keep.tile([P, 2, TOKEN_TILES, P, PACK], BF16, align_bytes=64)
        r_codes = keep.tile([P, 2, TOKEN_TILES, P], U32, align_bytes=64)
        r_scales = keep.tile([P, 2, TOKEN_TILES, P], U8, align_bytes=64)

        x_res, h, h_scaled, sum_sq, rms, rstd, h_t = {}, {}, {}, {}, {}, {}, {}
        raw, grouped_parts, codes, scales = {}, {}, {}, {}
        r_t, banks, gate_act = {}, {}, {}

        def load_tokens(tt):
            rows = slice(tt * P, (tt + 1) * P)
            x_res[tt] = raw_pool.tile([P, 2, H], BF16, tag="raw", name="x_res")
            h[tt] = raw_pool.tile([P, H], F32, tag="raw", name="h")
            h_scaled[tt] = raw_pool.tile([P, H], F32, tag="raw", name="h_scaled")
            sum_sq[tt] = small.tile([P, 2], F32, name="sum_sq")
            for cols in H_HALVES:
                nc.sync.dma_start(out=x_res[tt][:, 0, cols], in_=x_rows[rows, cols])
                nc.sync.dma_start(out=x_res[tt][:, 1, cols], in_=res_rows[rows, cols])

        def add_and_square(tt, half):
            cols = H_HALVES[half]
            nc.vector.tensor_tensor(
                out=h[tt][:, cols], in0=x_res[tt][:, 0, cols], in1=x_res[tt][:, 1, cols], op=ALU.add
            )
            nc.scalar.activation(
                out=h_scaled[tt][:, cols], in_=h[tt][:, cols], func=ACT.Square,
                accum_out=sum_sq[tt][:, half : half + 1],
            )

        def root_mean_square(tt):
            first_mean = small.tile([P, 1], F32, name="first_mean")
            nc.scalar.activation(
                out=first_mean[:], in_=sum_sq[tt][:, 0:1], func=ACT.Identity,
                scale=1.0 / H, bias=eps[:, 0:1],
            )
            rms[tt] = small.tile([P, 1], F32, name="rms")
            nc.scalar.activation(
                out=rms[tt][:], in_=sum_sq[tt][:, 1:2], func=ACT.Sqrt,
                scale=1.0 / H, bias=first_mean[:, 0:1],
            )

        def reciprocal_rms(tt):
            rstd[tt] = small.tile([P, 1], F32, name="rstd")
            nc.vector.reciprocal(rstd[tt][:], rms[tt][:])

        def transpose_tokens(tt):
            for g in range(H_PASSES):
                h_t[tt, g] = psum.tile([P, PACK, P], F32, tag="bank", name="h_t")
                for j in range(PACK):
                    k0 = K_PASS * g + P * j
                    nc.tensor.transpose(
                        h_t[tt, g][:, j, :], h_scaled[tt][:, k0 : k0 + P], ident[:]
                    )

        def apply_gain(tt):
            for g in range(H_PASSES):
                nc.vector.tensor_tensor(
                    out=n_grouped[:, tt, g, :, :],
                    in0=h_t[tt, g][:].rearrange("p j t -> p t j"),
                    in1=gain[:, PACK * g : PACK * (g + 1)].unsqueeze(1).to_broadcast([P, P, PACK]),
                    op=ALU.mult,
                )

        def quantise_tokens(tt):
            nc.vector.quantize_mx(
                out=n_codes[:, tt].rearrange("p g t -> p (g t)").bitcast(FP8X4),
                scales=n_scales[:, tt].rearrange("p g t -> p (g t)"),
                in_=n_grouped[:, tt].rearrange("p g t j -> p (g t j)"),
            )

        def load_v(m, piece):
            key = ("v", m, piece)
            raw[key] = raw_pool.tile([P, PACK, PIECE], BF16, tag="raw", name="raw_v")
            for half in range(2):
                nc.sync.dma_start(
                    out=raw[key][:, :, half * R : (half + 1) * R],
                    in_=v_views[m][:, 2 * piece + half, :, :],
                )
            codes[key] = v_codes[m][:, piece * PIECE : (piece + 1) * PIECE]
            scales[key] = v_scales[m][:, piece * PIECE : (piece + 1) * PIECE]

        def load_u(piece):
            if piece < U_PIECES:
                for m in (GATE, UP):
                    key = ("u", m, piece)
                    raw[key] = raw_pool.tile([P, PACK, PIECE], BF16, tag="raw", name="raw_u")
                    nc.sync.dma_start(
                        out=raw[key][:], in_=u_views[m][:, :, piece * PIECE : (piece + 1) * PIECE]
                    )

        def one_grouped_part(key):
            whole = grouped_pool.tile([P, PIECE, PACK], BF16, align_bytes=64, name="grouped")
            grouped_parts[key] = [(0, PIECE, whole)]

        def two_grouped_parts(key):
            first = up_first_pool.tile([P, HALF, PACK], BF16, align_bytes=64, name="up_first")
            second = up_second_pool.tile([P, HALF, PACK], BF16, align_bytes=64, name="up_second")
            grouped_parts[key] = [(0, HALF, first), (HALF, PIECE, second)]

        def grouped_columns(key, lo, hi):
            views = [
                part[:, lo - start : hi - start, :]
                for start, end, part in grouped_parts[key]
                if start <= lo and hi <= end
            ]
            return views[0]

        def regroup(copy, key, lo, hi):
            copy(
                out=grouped_columns(key, lo, hi).rearrange("p (c i) j -> p c j i", i=RUN),
                in_=raw[key][:, :, lo:hi].rearrange("p j (c i) -> p c j i", i=RUN),
            )

        def regroup_on_gpsimd(key, lo, hi):
            nc.gpsimd.tensor_scalar(
                out=grouped_columns(key, lo, hi),
                in0=raw[key][:, :, lo:hi].rearrange("p j c -> p c j"),
                scalar1=1.0, scalar2=0.0, op0=ALU.mult, op1=ALU.add,
            )

        def regroup_piece(copy, key):
            one_grouped_part(key)
            regroup(copy, key, 0, HALF)
            regroup(copy, key, HALF, PIECE)

        def quantise_piece(key):
            if key not in codes:
                codes[key] = u_pool.tile([P, PIECE], U32, align_bytes=64, name="u_codes")
                scales[key] = u_pool.tile([P, PIECE], U8, align_bytes=64, name="u_scales")
            for start, end, part in grouped_parts[key]:
                nc.vector.quantize_mx(
                    out=codes[key][:, start:end].bitcast(FP8X4),
                    scales=scales[key][:, start:end],
                    in_=part[:].rearrange("p c j -> p (c j)"),
                )

        def first_product(m, tt):
            r_t[m, tt] = psum.tile([P, PACK, P], F32, tag="bank", name="r_t")
            for j in range(PACK):
                for g in range(H_PASSES):
                    r_cols = slice(R * g + P * j, R * g + P * (j + 1))
                    nc.tensor.matmul_mx(
                        out=r_t[m, tt][:, j, :],
                        lhsT=v_codes[m][:, r_cols].bitcast(FP8X4),
                        lhsT_scale=v_scales[m][:, r_cols],
                        rhs=n_codes[:, tt, g, :].bitcast(FP8X4),
                        rhs_scale=n_scales[:, tt, g, :],
                        start=(g == 0),
                        stop=(g == H_PASSES - 1),
                    )

        def round_first_product(m, tt):
            nc.scalar.copy(
                out=r_grouped[:, m, tt, :, :], in_=r_t[m, tt][:].rearrange("p j t -> p t j")
            )

        def second_products(piece):
            for m in (GATE, UP):
                for tt in range(TOKEN_TILES):
                    for b in range(BANKS_PER_PIECE):
                        cols = slice(b * BANK, (b + 1) * BANK)
                        banks[m, tt, b] = psum.tile([P, BANK], F32, tag="bank", name="bank")
                        nc.tensor.matmul_mx(
                            out=banks[m, tt, b][:],
                            lhsT=r_codes[:, m, tt, :].bitcast(FP8X4),
                            lhsT_scale=r_scales[:, m, tt, :],
                            rhs=codes["u", m, piece][:, cols].bitcast(FP8X4),
                            rhs_scale=scales["u", m, piece][:, cols],
                            start=True,
                            stop=True,
                        )

        def silu_of_gate():
            for tt in range(TOKEN_TILES):
                for b in range(BANKS_PER_PIECE):
                    gate_act[tt, b] = act_pool.tile([P, BANK], F32, name="gate_act")
                    nc.scalar.activation(
                        out=gate_act[tt, b][:], in_=banks[GATE, tt, b][:], func=ACT.Silu
                    )

        def multiply_and_store(piece):
            for tt in range(TOKEN_TILES):
                product = product_pool.tile([P, PIECE], F32, name="product")
                for b in range(BANKS_PER_PIECE):
                    nc.vector.tensor_tensor(
                        out=product[:, b * BANK : (b + 1) * BANK],
                        in0=gate_act[tt, b][:], in1=banks[UP, tt, b][:], op=ALU.mult,
                    )
                nc.sync.dma_start(
                    out=out_rows[tt * P : (tt + 1) * P, piece * PIECE : (piece + 1) * PIECE],
                    in_=product[:],
                )

        eps = const.tile([P, 1], F32)
        nc.vector.memset(eps[:], EPS)
        warm = const.tile([P, 2], F32)
        nc.scalar.sqrt(warm[:, 0:1], eps[:])
        ident = const.tile([P, P], F32)
        make_identity(nc, ident[:])
        gain_rows = const.tile([P, P], BF16)
        nc.vector.memset(gain_rows[:], 0.0)

        on_vector = nc.vector.tensor_copy
        on_scalar = nc.scalar.copy
        load_tokens(0)
        load_tokens(1)
        nc.sync.dma_start(out=gain_rows[0 : H // P, :], in_=ln_w.rearrange("(c p) -> c p", p=P))
        for m in (GATE, UP):
            for piece in range(V_PIECES):
                load_v(m, piece)
        for tt in range(TOKEN_TILES):
            add_and_square(tt, 0)
            add_and_square(tt, 1)
            root_mean_square(tt)
        gain_rows_f32 = const.tile([P, P], F32)
        nc.vector.tensor_copy(out=gain_rows_f32[:], in_=gain_rows[:])
        gain_bank = psum.tile([P, P], F32, tag="bank")
        nc.tensor.transpose(gain_bank[:], gain_rows_f32[:], ident[:])
        gain = const.tile([P, H // P], F32)
        nc.vector.tensor_copy(out=gain[:], in_=gain_bank[:, 0 : H // P])
        load_u(0)
        load_u(1)
        reciprocal_rms(0)
        nc.vector.tensor_scalar_mul(out=h_scaled[0][:], in0=h[0][:], scalar1=rstd[0][:, 0:1])
        transpose_tokens(0)
        regroup_piece(on_vector, ("v", GATE, 0))
        reciprocal_rms(1)
        nc.scalar.activation(out=h_scaled[1][:], in_=h[1][:], func=ACT.Copy, scale=rstd[1][:, 0:1])
        nc.scalar.activation(out=warm[:, 1:2], in_=eps[:], func=ACT.Silu)
        transpose_tokens(1)
        regroup_piece(on_vector, ("v", GATE, 1))
        regroup_piece(on_scalar, ("v", UP, 0))
        apply_gain(0)
        apply_gain(1)
        quantise_tokens(0)
        quantise_tokens(1)
        quantise_piece(("v", GATE, 0))
        quantise_piece(("v", GATE, 1))
        first_product(GATE, 0)
        first_product(GATE, 1)
        regroup_piece(on_scalar, ("v", UP, 1))
        load_u(2)
        load_u(3)
        quantise_piece(("v", UP, 0))
        regroup_piece(on_vector, ("u", GATE, 0))
        quantise_piece(("v", UP, 1))
        first_product(UP, 0)
        first_product(UP, 1)
        round_first_product(GATE, 0)
        round_first_product(GATE, 1)
        two_grouped_parts(("u", UP, 0))
        regroup(on_scalar, ("u", UP, 0), 0, HALF)
        regroup(on_scalar, ("u", UP, 0), HALF, PIECE)
        load_u(4)
        quantise_piece(("u", GATE, 0))
        regroup_piece(on_vector, ("u", GATE, 1))
        round_first_product(UP, 0)
        round_first_product(UP, 1)
        quantise_piece(("u", UP, 0))
        nc.vector.quantize_mx(
            out=r_codes[:].rearrange("p m a t -> p (m a t)").bitcast(FP8X4),
            scales=r_scales[:].rearrange("p m a t -> p (m a t)"),
            in_=r_grouped[:].rearrange("p m a t j -> p (m a t j)"),
        )
        two_grouped_parts(("u", UP, 1))
        regroup(on_scalar, ("u", UP, 1), 0, HALF)
        regroup(on_scalar, ("u", UP, 1), HALF, PIECE)

        for s in range(U_PIECES):
            load_u(s + LOADS_AHEAD)
            second_products(s)
            silu_of_gate()
            if s + 2 < U_PIECES:
                one_grouped_part(("u", GATE, s + 2))
                regroup(on_vector, ("u", GATE, s + 2), 0, GATE_VECTOR_COLS)
                regroup(on_scalar, ("u", GATE, s + 2), GATE_VECTOR_COLS, PIECE)
            if s + 1 < U_PIECES:
                quantise_piece(("u", GATE, s + 1))
                quantise_piece(("u", UP, s + 1))
            if s + 2 < U_PIECES:
                two_grouped_parts(("u", UP, s + 2))
                regroup(on_scalar, ("u", UP, s + 2), 0, HALF)
                regroup_on_gpsimd(("u", UP, s + 2), HALF, PIECE)
            multiply_and_store(s)
